import numpy as np
import ml_dtypes

BF16 = ml_dtypes.bfloat16


def bf(x):
    return np.asarray(x, np.float32).astype(BF16)


def f32(x):
    return np.asarray(x, np.float32)


def f64(x):
    return np.asarray(x).astype(np.float64)


def striped(idx):
    return np.tile(idx.reshape(-1, 16).T, (8, 1))


F, H, K, IN, MID, C, S, N = 16, 48, 128, 129, 128, 128, 4096, 2048


def setup_inputs():
    return {
        "base": f32(np.random.standard_normal((C, S))),
        "dst_feat": bf(np.random.standard_normal((F, N))),
        "dst_hidden": bf(np.random.standard_normal((H, N))),
        "src_feat": bf(np.random.standard_normal((F, N))),
        "src_hidden": bf(np.random.standard_normal((H, N))),
        "edge_feat": f32(np.random.standard_normal((1, N))),
        "w1": bf(np.random.standard_normal((K, MID)) / np.sqrt(IN)),
        "w_edge": f32(np.random.standard_normal((MID, 1)) / np.sqrt(IN)),
        "b1": f32(0.1 * np.random.standard_normal((MID, 1))),
        "w2": bf(np.random.standard_normal((MID, C)) / np.sqrt(MID)),
        "b2": f32(0.1 * np.random.standard_normal((C, 1))),
        "offs": striped(np.random.permutation(S)[:N]),
    }


def reference(base, dst_feat, dst_hidden, src_feat, src_hidden, edge_feat, w1, w_edge, b1, w2, b2, offs):
    idx = offs[:16].T.reshape(-1)
    x = np.concatenate([f64(dst_feat), f64(dst_hidden), f64(src_feat), f64(src_hidden)], axis=0)
    h = np.maximum(f64(w1).T @ x + f64(w_edge) * f64(edge_feat) + f64(b1), 0.0)
    out = f64(base).copy()
    out[:, idx] = f64(w2).T @ h + f64(b2)
    return out

@@ -1,0 +1,75 @@
+import concourse.mybir as mybir
+
+F32, BF16, U16 = mybir.dt.float32, mybir.dt.bfloat16, mybir.dt.uint16
+ADD, MULT = mybir.AluOpType.add, mybir.AluOpType.mult
+RELU = mybir.ActivationFunctionType.Relu
+
+P = 128
+N = 2048
+S = 4096
+PIECE = 512
+PIECES = N // PIECE
+
+FLOPS = 2 * N * (P * P + P + P * P)
+BYTES = 4 * P * S + 4 * P * (S - N) + 2 * P * N + 4 * N + 2 * 2 * P * P + 3 * 4 * P + 2 * P * (N // 16)
+
+
+def tile_edgenetwork_kernel(
+    tc, base, dst_feat, dst_hidden, src_feat, src_hidden, edge_feat, w1, w_edge, b1, w2, b2, offs, out
+):
+    nc = tc.nc
+    with (
+        tc.tile_pool(name="held", bufs=1) as held,
+        tc.psum_pool(name="psum", bufs=PIECES) as psum,
+    ):
+        offsets = held.tile([P, N // 16], U16, name="offsets")
+        window = held.tile([P, S], F32, name="window")
+        x = held.tile([P, N], BF16, name="x")
+        edge_rows = held.tile([P, N], F32, name="edge_rows")
+        w1_sb = held.tile([P, P], BF16, name="w1_sb")
+        w2_sb = held.tile([P, P], BF16, name="w2_sb")
+        w_edge_col = held.tile([P, 1], F32, name="w_edge_col")
+        b1_col = held.tile([P, 1], F32, name="b1_col")
+        b2_col = held.tile([P, 1], F32, name="b2_col")
+        pre = held.tile([P, N], F32, name="pre")
+        h = held.tile([P, N], BF16, name="h")
+        y = held.tile([P, N], F32, name="y")
+        b2_rows = held.tile([P, N], F32, name="b2_rows")
+        scratch = held.tile([P, 1], F32, name="scratch")
+
+        nc.sync.dma_start(w_edge_col[:], w_edge)
+        nc.scalar.dma_start(w1_sb[:], w1)
+        nc.sync.dma_start(x[0:16, :], dst_feat)
+        nc.sync.dma_start(x[16:64, :], dst_hidden)
+        nc.scalar.dma_start(x[64:80, :], src_feat)
+        nc.scalar.dma_start(x[80:128, :], src_hidden)
+        nc.scalar.dma_start(b1_col[:], b1)
+        for k in range(PIECES):
+            cols = slice(k * PIECE, (k + 1) * PIECE)
+            queue = nc.sync if k % 2 == 0 else nc.scalar
+            queue.dma_start(edge_rows[:, cols], edge_feat[:, cols].broadcast_to([P, PIECE]))
+        nc.scalar.dma_start(w2_sb[:], w2)
+        nc.scalar.dma_start(b2_col[:], b2)
+        nc.sync.dma_start(offsets[:], offs)
+        nc.sync.dma_start(window[:, 0 : S // 2], base[:, 0 : S // 2])
+        nc.scalar.dma_start(window[:, S // 2 : S], base[:, S // 2 : S])
+
+        nc.vector.memset(scratch[:], 0.0)
+        nc.scalar.activation(scratch[:], scratch[:], RELU)
+
+        nc.gpsimd.tensor_copy(b2_rows[:], b2_col[:].to_broadcast([P, N]))
+
+        for k in range(PIECES):
+            cols = slice(k * PIECE, (k + 1) * PIECE)
+            layer1 = psum.tile([P, PIECE], F32, name="layer1")
+            nc.tensor.matmul(layer1[:], w1_sb[:], x[:, cols], start=True, stop=True)
+            nc.vector.scalar_tensor_tensor(pre[:, cols], edge_rows[:, cols], w_edge_col[:], layer1[:], MULT, ADD)
+            nc.scalar.activation(h[:, cols], pre[:, cols], RELU, bias=b1_col[:])
+            layer2 = psum.tile([P, PIECE], F32, name="layer2")
+            nc.tensor.matmul(layer2[:], w2_sb[:], h[:, cols], start=True, stop=True)
+            nc.vector.tensor_copy(y[:, cols], layer2[:])
+
+        nc.vector.tensor_tensor(window[:].indirect(offsets[:]), y[:], b2_rows[:], ADD)
+
+        nc.sync.dma_start(out[:, 0 : S // 2], window[:, 0 : S // 2])
+        nc.scalar.dma_start(out[:, S // 2 : S], window[:, S // 2 : S])

@@ -35,27 +35,23 @@ def tile_edgenetwork_kernel(
         h = held.tile([P, N], BF16, name="h")
         y = held.tile([P, N], F32, name="y")
         b2_rows = held.tile([P, N], F32, name="b2_rows")
-        scratch = held.tile([P, 1], F32, name="scratch")
 
-        nc.sync.dma_start(w_edge_col[:], w_edge)
+        nc.gpsimd.dma_start(w_edge_col[:], w_edge)
+        nc.gpsimd.dma_start(b1_col[:], b1)
+        nc.gpsimd.dma_start(b2_col[:], b2)
         nc.scalar.dma_start(w1_sb[:], w1)
         nc.sync.dma_start(x[0:16, :], dst_feat)
         nc.sync.dma_start(x[16:64, :], dst_hidden)
         nc.scalar.dma_start(x[64:80, :], src_feat)
         nc.scalar.dma_start(x[80:128, :], src_hidden)
-        nc.scalar.dma_start(b1_col[:], b1)
         for k in range(PIECES):
             cols = slice(k * PIECE, (k + 1) * PIECE)
             queue = nc.sync if k % 2 == 0 else nc.scalar
             queue.dma_start(edge_rows[:, cols], edge_feat[:, cols].broadcast_to([P, PIECE]))
         nc.scalar.dma_start(w2_sb[:], w2)
-        nc.scalar.dma_start(b2_col[:], b2)
         nc.sync.dma_start(offsets[:], offs)
         nc.sync.dma_start(window[:, 0 : S // 2], base[:, 0 : S // 2])
         nc.scalar.dma_start(window[:, S // 2 : S], base[:, S // 2 : S])
-
-        nc.vector.memset(scratch[:], 0.0)
-        nc.scalar.activation(scratch[:], scratch[:], RELU)
 
         nc.gpsimd.tensor_copy(b2_rows[:], b2_col[:].to_broadcast([P, N]))
 

@@ -35,23 +35,25 @@ def tile_edgenetwork_kernel(
         h = held.tile([P, N], BF16, name="h")
         y = held.tile([P, N], F32, name="y")
         b2_rows = held.tile([P, N], F32, name="b2_rows")
+        scratch = held.tile([P, 1], F32, name="scratch")
 
-        nc.gpsimd.dma_start(w_edge_col[:], w_edge)
-        nc.gpsimd.dma_start(b1_col[:], b1)
         nc.gpsimd.dma_start(b2_col[:], b2)
         nc.scalar.dma_start(w1_sb[:], w1)
         nc.sync.dma_start(x[0:16, :], dst_feat)
-        nc.sync.dma_start(x[16:64, :], dst_hidden)
         nc.scalar.dma_start(x[64:80, :], src_feat)
+        nc.sync.dma_start(x[16:64, :], dst_hidden)
         nc.scalar.dma_start(x[80:128, :], src_hidden)
+        nc.scalar.dma_start(w_edge_col[:], w_edge)
+        nc.scalar.dma_start(b1_col[:], b1)
         for k in range(PIECES):
             cols = slice(k * PIECE, (k + 1) * PIECE)
-            queue = nc.sync if k % 2 == 0 else nc.scalar
-            queue.dma_start(edge_rows[:, cols], edge_feat[:, cols].broadcast_to([P, PIECE]))
-        nc.scalar.dma_start(w2_sb[:], w2)
+            nc.sync.dma_start(edge_rows[:, cols], edge_feat[:, cols].broadcast_to([P, PIECE]))
+        nc.sync.dma_start(w2_sb[:], w2)
         nc.sync.dma_start(offsets[:], offs)
-        nc.sync.dma_start(window[:, 0 : S // 2], base[:, 0 : S // 2])
-        nc.scalar.dma_start(window[:, S // 2 : S], base[:, S // 2 : S])
+        nc.sync.dma_start(window[:], base)
+
+        nc.vector.memset(scratch[:], 0.0)
+        nc.scalar.activation(scratch[:], scratch[:], RELU)
 
         nc.gpsimd.tensor_copy(b2_rows[:], b2_col[:].to_broadcast([P, N]))
 

@@ -39,16 +39,15 @@ def tile_edgenetwork_kernel(
 
         nc.gpsimd.dma_start(b2_col[:], b2)
         nc.scalar.dma_start(w1_sb[:], w1)
+        nc.scalar.dma_start(w_edge_col[:], w_edge)
         nc.sync.dma_start(x[0:16, :], dst_feat)
         nc.scalar.dma_start(x[64:80, :], src_feat)
         nc.sync.dma_start(x[16:64, :], dst_hidden)
         nc.scalar.dma_start(x[80:128, :], src_hidden)
-        nc.scalar.dma_start(w_edge_col[:], w_edge)
+        for half in (slice(0, N // 2), slice(N // 2, N)):
+            nc.sync.dma_start(edge_rows[:, half], edge_feat[:, half].broadcast_to([P, N // 2]))
         nc.scalar.dma_start(b1_col[:], b1)
-        for k in range(PIECES):
-            cols = slice(k * PIECE, (k + 1) * PIECE)
-            nc.sync.dma_start(edge_rows[:, cols], edge_feat[:, cols].broadcast_to([P, PIECE]))
-        nc.sync.dma_start(w2_sb[:], w2)
+        nc.scalar.dma_start(w2_sb[:], w2)
         nc.sync.dma_start(offsets[:], offs)
         nc.sync.dma_start(window[:], base)
 

@@ -42,10 +42,10 @@ def tile_edgenetwork_kernel(
         nc.scalar.dma_start(w_edge_col[:], w_edge)
         nc.sync.dma_start(x[0:16, :], dst_feat)
         nc.scalar.dma_start(x[64:80, :], src_feat)
+        nc.sync.dma_start(edge_rows[:, 0 : N // 2], edge_feat[:, 0 : N // 2].broadcast_to([P, N // 2]))
         nc.sync.dma_start(x[16:64, :], dst_hidden)
         nc.scalar.dma_start(x[80:128, :], src_hidden)
-        for half in (slice(0, N // 2), slice(N // 2, N)):
-            nc.sync.dma_start(edge_rows[:, half], edge_feat[:, half].broadcast_to([P, N // 2]))
+        nc.sync.dma_start(edge_rows[:, N // 2 : N], edge_feat[:, N // 2 : N].broadcast_to([P, N // 2]))
         nc.scalar.dma_start(b1_col[:], b1)
         nc.scalar.dma_start(w2_sb[:], w2)
         nc.sync.dma_start(offsets[:], offs)

@@ -35,7 +35,6 @@ def tile_edgenetwork_kernel(
         h = held.tile([P, N], BF16, name="h")
         y = held.tile([P, N], F32, name="y")
         b2_rows = held.tile([P, N], F32, name="b2_rows")
-        scratch = held.tile([P, 1], F32, name="scratch")
 
         nc.gpsimd.dma_start(b2_col[:], b2)
         nc.scalar.dma_start(w1_sb[:], w1)
@@ -50,9 +49,6 @@ def tile_edgenetwork_kernel(
         nc.scalar.dma_start(w2_sb[:], w2)
         nc.sync.dma_start(offsets[:], offs)
         nc.sync.dma_start(window[:], base)
-
-        nc.vector.memset(scratch[:], 0.0)
-        nc.scalar.activation(scratch[:], scratch[:], RELU)
 
         nc.gpsimd.tensor_copy(b2_rows[:], b2_col[:].to_broadcast([P, N]))
 

@@ -1,7 +1,7 @@
 import concourse.mybir as mybir
 
 F32, BF16, U16 = mybir.dt.float32, mybir.dt.bfloat16, mybir.dt.uint16
-ADD, MULT = mybir.AluOpType.add, mybir.AluOpType.mult
+ADD, MULT, MAX = mybir.AluOpType.add, mybir.AluOpType.mult, mybir.AluOpType.max
 RELU = mybir.ActivationFunctionType.Relu
 
 P = 128
@@ -9,6 +9,8 @@ N = 2048
 S = 4096
 PIECE = 512
 PIECES = N // PIECE
+LAST = PIECES - 1
+SPREAD = LAST * PIECE
 
 FLOPS = 2 * N * (P * P + P + P * P)
 BYTES = 4 * P * S + 4 * P * (S - N) + 2 * P * N + 4 * N + 2 * 2 * P * P + 3 * 4 * P + 2 * P * (N // 16)
@@ -25,42 +27,54 @@ def tile_edgenetwork_kernel(
         offsets = held.tile([P, N // 16], U16, name="offsets")
         window = held.tile([P, S], F32, name="window")
         x = held.tile([P, N], BF16, name="x")
-        edge_rows = held.tile([P, N], F32, name="edge_rows")
+        edge_rows = held.tile([P, SPREAD], F32, name="edge_rows")
+        edge_tail = held.tile([1, PIECE], F32, name="edge_tail")
         w1_sb = held.tile([P, P], BF16, name="w1_sb")
         w2_sb = held.tile([P, P], BF16, name="w2_sb")
+        w_edge_row = held.tile([1, P], F32, name="w_edge_row")
         w_edge_col = held.tile([P, 1], F32, name="w_edge_col")
         b1_col = held.tile([P, 1], F32, name="b1_col")
         b2_col = held.tile([P, 1], F32, name="b2_col")
-        pre = held.tile([P, N], F32, name="pre")
+        pre = held.tile([P, SPREAD], F32, name="pre")
         h = held.tile([P, N], BF16, name="h")
         y = held.tile([P, N], F32, name="y")
         b2_rows = held.tile([P, N], F32, name="b2_rows")
 
-        nc.gpsimd.dma_start(b2_col[:], b2)
+        nc.gpsimd.dma_start(b1_col[:], b1)
+        nc.sync.dma_start(edge_tail[:], edge_feat[:, SPREAD:N])
+        nc.scalar.dma_start(w_edge_row[:], w_edge.rearrange("m o -> o m"))
         nc.scalar.dma_start(w1_sb[:], w1)
-        nc.scalar.dma_start(w_edge_col[:], w_edge)
         nc.sync.dma_start(x[0:16, :], dst_feat)
         nc.scalar.dma_start(x[64:80, :], src_feat)
-        nc.sync.dma_start(edge_rows[:, 0 : N // 2], edge_feat[:, 0 : N // 2].broadcast_to([P, N // 2]))
+        nc.scalar.dma_start(edge_rows[:, 0:PIECE], edge_feat[:, 0:PIECE].broadcast_to([P, PIECE]))
         nc.sync.dma_start(x[16:64, :], dst_hidden)
         nc.scalar.dma_start(x[80:128, :], src_hidden)
-        nc.sync.dma_start(edge_rows[:, N // 2 : N], edge_feat[:, N // 2 : N].broadcast_to([P, N // 2]))
-        nc.scalar.dma_start(b1_col[:], b1)
-        nc.scalar.dma_start(w2_sb[:], w2)
+        nc.scalar.dma_start(w_edge_col[:], w_edge)
+        nc.scalar.dma_start(b2_col[:], b2)
+        nc.sync.dma_start(edge_rows[:, PIECE:SPREAD], edge_feat[:, PIECE:SPREAD].broadcast_to([P, SPREAD - PIECE]))
+        nc.sync.dma_start(w2_sb[:], w2)
         nc.sync.dma_start(offsets[:], offs)
         nc.sync.dma_start(window[:], base)
 
-        nc.gpsimd.tensor_copy(b2_rows[:], b2_col[:].to_broadcast([P, N]))
+        nc.gpsimd.tensor_scalar(b2_rows[:], b2_col[:].to_broadcast([P, N]), 1.0, 0.0, MULT, ADD)
+
+        layer1 = [psum.tile([P, PIECE], F32, name="layer1") for k in range(PIECES)]
+        nc.tensor.matmul(layer1[LAST][:], w_edge_row[:], edge_tail[:], start=True, stop=False)
 
         for k in range(PIECES):
             cols = slice(k * PIECE, (k + 1) * PIECE)
-            layer1 = psum.tile([P, PIECE], F32, name="layer1")
-            nc.tensor.matmul(layer1[:], w1_sb[:], x[:, cols], start=True, stop=True)
-            nc.vector.scalar_tensor_tensor(pre[:, cols], edge_rows[:, cols], w_edge_col[:], layer1[:], MULT, ADD)
-            nc.scalar.activation(h[:, cols], pre[:, cols], RELU, bias=b1_col[:])
+            nc.tensor.matmul(layer1[k][:], w1_sb[:], x[:, cols], start=(k != LAST), stop=True)
+            if k == LAST:
+                nc.vector.tensor_scalar(h[:, cols], layer1[k][:], b1_col[:], 0.0, ADD, MAX)
+            else:
+                nc.vector.scalar_tensor_tensor(pre[:, cols], edge_rows[:, cols], w_edge_col[:], layer1[k][:], MULT, ADD)
+                nc.scalar.activation(h[:, cols], pre[:, cols], RELU, bias=b1_col[:])
             layer2 = psum.tile([P, PIECE], F32, name="layer2")
             nc.tensor.matmul(layer2[:], w2_sb[:], h[:, cols], start=True, stop=True)
-            nc.vector.tensor_copy(y[:, cols], layer2[:])
+            if k % 2 == 1:
+                nc.vector.tensor_copy(y[:, cols], layer2[:])
+            else:
+                nc.scalar.copy(y[:, cols], layer2[:])
 
         nc.vector.tensor_tensor(window[:].indirect(offsets[:]), y[:], b2_rows[:], ADD)
 

@@ -33,6 +33,7 @@ def tile_edgenetwork_kernel(
         w2_sb = held.tile([P, P], BF16, name="w2_sb")
         w_edge_row = held.tile([1, P], F32, name="w_edge_row")
         w_edge_col = held.tile([P, 1], F32, name="w_edge_col")
+        warm = held.tile([1, P], F32, name="warm")
         b1_col = held.tile([P, 1], F32, name="b1_col")
         b2_col = held.tile([P, 1], F32, name="b2_col")
         pre = held.tile([P, SPREAD], F32, name="pre")
@@ -40,7 +41,7 @@ def tile_edgenetwork_kernel(
         y = held.tile([P, N], F32, name="y")
         b2_rows = held.tile([P, N], F32, name="b2_rows")
 
-        nc.gpsimd.dma_start(b1_col[:], b1)
+        nc.gpsimd.dma_start(b2_col[:], b2)
         nc.sync.dma_start(edge_tail[:], edge_feat[:, SPREAD:N])
         nc.scalar.dma_start(w_edge_row[:], w_edge.rearrange("m o -> o m"))
         nc.scalar.dma_start(w1_sb[:], w1)
@@ -50,11 +51,13 @@ def tile_edgenetwork_kernel(
         nc.sync.dma_start(x[16:64, :], dst_hidden)
         nc.scalar.dma_start(x[80:128, :], src_hidden)
         nc.scalar.dma_start(w_edge_col[:], w_edge)
-        nc.scalar.dma_start(b2_col[:], b2)
+        nc.scalar.dma_start(b1_col[:], b1)
         nc.sync.dma_start(edge_rows[:, PIECE:SPREAD], edge_feat[:, PIECE:SPREAD].broadcast_to([P, SPREAD - PIECE]))
         nc.sync.dma_start(w2_sb[:], w2)
         nc.sync.dma_start(offsets[:], offs)
         nc.sync.dma_start(window[:], base)
+
+        nc.scalar.activation(warm[:], w_edge_row[:], RELU)
 
         nc.gpsimd.tensor_scalar(b2_rows[:], b2_col[:].to_broadcast([P, N]), 1.0, 0.0, MULT, ADD)
 

@@ -22,7 +22,9 @@ def tile_edgenetwork_kernel(
     nc = tc.nc
     with (
         tc.tile_pool(name="held", bufs=1) as held,
-        tc.psum_pool(name="psum", bufs=PIECES) as psum,
+        tc.psum_pool(name="psum1", bufs=PIECES) as psum1,
+        tc.psum_pool(name="psum2", bufs=PIECES - 1) as psum2,
+        tc.psum_pool(name="psum3", bufs=1) as psum3,
     ):
         offsets = held.tile([P, N // 16], U16, name="offsets")
         window = held.tile([P, S], F32, name="window")
@@ -33,7 +35,7 @@ def tile_edgenetwork_kernel(
         w2_sb = held.tile([P, P], BF16, name="w2_sb")
         w_edge_row = held.tile([1, P], F32, name="w_edge_row")
         w_edge_col = held.tile([P, 1], F32, name="w_edge_col")
-        warm = held.tile([1, P], F32, name="warm")
+        one = held.tile([1, 1], F32, name="one")
         b1_col = held.tile([P, 1], F32, name="b1_col")
         b2_col = held.tile([P, 1], F32, name="b2_col")
         pre = held.tile([P, SPREAD], F32, name="pre")
@@ -42,37 +44,38 @@ def tile_edgenetwork_kernel(
         b2_rows = held.tile([P, N], F32, name="b2_rows")
 
         nc.gpsimd.dma_start(b2_col[:], b2)
-        nc.sync.dma_start(edge_tail[:], edge_feat[:, SPREAD:N])
-        nc.scalar.dma_start(w_edge_row[:], w_edge.rearrange("m o -> o m"))
-        nc.scalar.dma_start(w1_sb[:], w1)
         nc.sync.dma_start(x[0:16, :], dst_feat)
-        nc.scalar.dma_start(x[64:80, :], src_feat)
-        nc.scalar.dma_start(edge_rows[:, 0:PIECE], edge_feat[:, 0:PIECE].broadcast_to([P, PIECE]))
+        nc.scalar.dma_start(w1_sb[:], w1)
+        nc.sync.dma_start(x[64:80, :], src_feat)
+        nc.scalar.dma_start(w_edge_row[:], w_edge.rearrange("m o -> o m"))
         nc.sync.dma_start(x[16:64, :], dst_hidden)
-        nc.scalar.dma_start(x[80:128, :], src_hidden)
-        nc.scalar.dma_start(w_edge_col[:], w_edge)
         nc.scalar.dma_start(b1_col[:], b1)
-        nc.sync.dma_start(edge_rows[:, PIECE:SPREAD], edge_feat[:, PIECE:SPREAD].broadcast_to([P, SPREAD - PIECE]))
-        nc.sync.dma_start(w2_sb[:], w2)
+        nc.scalar.dma_start(x[80:128, :], src_hidden)
+        nc.scalar.dma_start(edge_rows[:], edge_feat[:, 0:SPREAD].broadcast_to([P, SPREAD]))
+        nc.scalar.dma_start(w2_sb[:], w2)
+        nc.sync.dma_start(edge_tail[:], edge_feat[:, SPREAD:N])
         nc.sync.dma_start(offsets[:], offs)
         nc.sync.dma_start(window[:], base)
 
-        nc.scalar.activation(warm[:], w_edge_row[:], RELU)
+        nc.vector.memset(one[:], 1.0)
+        w_edge_turned = psum3.tile([P, 1], F32, name="w_edge_turned")
+        nc.tensor.matmul(w_edge_turned[:], w_edge_row[:], one[:], start=True, stop=True)
+        nc.vector.tensor_copy(w_edge_col[:], w_edge_turned[:])
 
-        nc.gpsimd.tensor_scalar(b2_rows[:], b2_col[:].to_broadcast([P, N]), 1.0, 0.0, MULT, ADD)
-
-        layer1 = [psum.tile([P, PIECE], F32, name="layer1") for k in range(PIECES)]
-        nc.tensor.matmul(layer1[LAST][:], w_edge_row[:], edge_tail[:], start=True, stop=False)
+        nc.gpsimd.tensor_copy(b2_rows[:], b2_col[:].to_broadcast([P, N]))
 
         for k in range(PIECES):
             cols = slice(k * PIECE, (k + 1) * PIECE)
-            nc.tensor.matmul(layer1[k][:], w1_sb[:], x[:, cols], start=(k != LAST), stop=True)
+            layer1 = psum1.tile([P, PIECE], F32, name="layer1")
             if k == LAST:
-                nc.vector.tensor_scalar(h[:, cols], layer1[k][:], b1_col[:], 0.0, ADD, MAX)
+                nc.tensor.matmul(layer1[:], w1_sb[:], x[:, cols], start=True, stop=False)
+                nc.tensor.matmul(layer1[:], w_edge_row[:], edge_tail[:], start=False, stop=True)
+                nc.vector.tensor_scalar(h[:, cols], layer1[:], b1_col[:], 0.0, ADD, MAX)
             else:
-                nc.vector.scalar_tensor_tensor(pre[:, cols], edge_rows[:, cols], w_edge_col[:], layer1[k][:], MULT, ADD)
+                nc.tensor.matmul(layer1[:], w1_sb[:], x[:, cols], start=True, stop=True)
+                nc.vector.scalar_tensor_tensor(pre[:, cols], edge_rows[:, cols], w_edge_col[:], layer1[:], MULT, ADD)
                 nc.scalar.activation(h[:, cols], pre[:, cols], RELU, bias=b1_col[:])
-            layer2 = psum.tile([P, PIECE], F32, name="layer2")
+            layer2 = psum2.tile([P, PIECE], F32, name="layer2")
             nc.tensor.matmul(layer2[:], w2_sb[:], h[:, cols], start=True, stop=True)
             if k % 2 == 1:
                 nc.vector.tensor_copy(y[:, cols], layer2[:])

@@ -34,9 +34,9 @@ def tile_edgenetwork_kernel(
         w1_sb = held.tile([P, P], BF16, name="w1_sb")
         w2_sb = held.tile([P, P], BF16, name="w2_sb")
         w_edge_row = held.tile([1, P], F32, name="w_edge_row")
-        w_edge_col = held.tile([P, 1], F32, name="w_edge_col")
+        b1_row = held.tile([1, P], F32, name="b1_row")
         one = held.tile([1, 1], F32, name="one")
-        b1_col = held.tile([P, 1], F32, name="b1_col")
+        columns = held.tile([P, 2], F32, name="columns")
         b2_col = held.tile([P, 1], F32, name="b2_col")
         pre = held.tile([P, SPREAD], F32, name="pre")
         h = held.tile([P, N], BF16, name="h")
@@ -49,7 +49,7 @@ def tile_edgenetwork_kernel(
         nc.sync.dma_start(x[64:80, :], src_feat)
         nc.scalar.dma_start(w_edge_row[:], w_edge.rearrange("m o -> o m"))
         nc.sync.dma_start(x[16:64, :], dst_hidden)
-        nc.scalar.dma_start(b1_col[:], b1)
+        nc.scalar.dma_start(b1_row[:], b1.rearrange("m o -> o m"))
         nc.scalar.dma_start(x[80:128, :], src_hidden)
         nc.scalar.dma_start(edge_rows[:], edge_feat[:, 0:SPREAD].broadcast_to([P, SPREAD]))
         nc.scalar.dma_start(w2_sb[:], w2)
@@ -58,9 +58,12 @@ def tile_edgenetwork_kernel(
         nc.sync.dma_start(window[:], base)
 
         nc.vector.memset(one[:], 1.0)
-        w_edge_turned = psum3.tile([P, 1], F32, name="w_edge_turned")
-        nc.tensor.matmul(w_edge_turned[:], w_edge_row[:], one[:], start=True, stop=True)
-        nc.vector.tensor_copy(w_edge_col[:], w_edge_turned[:])
+        turned = psum3.tile([P, 2], F32, name="turned")
+        nc.tensor.matmul(turned[:, 0:1], w_edge_row[:], one[:], start=True, stop=True)
+        nc.tensor.matmul(turned[:, 1:2], b1_row[:], one[:], start=True, stop=True)
+        nc.vector.tensor_copy(columns[:], turned[:])
+        w_edge_col = columns[:, 0:1]
+        b1_col = columns[:, 1:2]
 
         nc.gpsimd.tensor_copy(b2_rows[:], b2_col[:].to_broadcast([P, N]))
 
@@ -70,11 +73,11 @@ def tile_edgenetwork_kernel(
             if k == LAST:
                 nc.tensor.matmul(layer1[:], w1_sb[:], x[:, cols], start=True, stop=False)
                 nc.tensor.matmul(layer1[:], w_edge_row[:], edge_tail[:], start=False, stop=True)
-                nc.vector.tensor_scalar(h[:, cols], layer1[:], b1_col[:], 0.0, ADD, MAX)
+                nc.vector.tensor_scalar(h[:, cols], layer1[:], b1_col, 0.0, ADD, MAX)
             else:
                 nc.tensor.matmul(layer1[:], w1_sb[:], x[:, cols], start=True, stop=True)
-                nc.vector.scalar_tensor_tensor(pre[:, cols], edge_rows[:, cols], w_edge_col[:], layer1[:], MULT, ADD)
-                nc.scalar.activation(h[:, cols], pre[:, cols], RELU, bias=b1_col[:])
+                nc.vector.scalar_tensor_tensor(pre[:, cols], edge_rows[:, cols], w_edge_col, layer1[:], MULT, ADD)
+                nc.scalar.activation(h[:, cols], pre[:, cols], RELU, bias=b1_col)
             layer2 = psum2.tile([P, PIECE], F32, name="layer2")
             nc.tensor.matmul(layer2[:], w2_sb[:], h[:, cols], start=True, stop=True)
             if k % 2 == 1:

@@ -22,9 +22,7 @@ def tile_edgenetwork_kernel(
     nc = tc.nc
     with (
         tc.tile_pool(name="held", bufs=1) as held,
-        tc.psum_pool(name="psum1", bufs=PIECES) as psum1,
-        tc.psum_pool(name="psum2", bufs=PIECES - 1) as psum2,
-        tc.psum_pool(name="psum3", bufs=1) as psum3,
+        tc.psum_pool(name="psum", bufs=PIECES) as psum,
     ):
         offsets = held.tile([P, N // 16], U16, name="offsets")
         window = held.tile([P, S], F32, name="window")
@@ -58,7 +56,7 @@ def tile_edgenetwork_kernel(
         nc.sync.dma_start(window[:], base)
 
         nc.vector.memset(one[:], 1.0)
-        turned = psum3.tile([P, 2], F32, name="turned")
+        turned = psum.tile([P, 2], F32, name="turned", tag="layer2")
         nc.tensor.matmul(turned[:, 0:1], w_edge_row[:], one[:], start=True, stop=True)
         nc.tensor.matmul(turned[:, 1:2], b1_row[:], one[:], start=True, stop=True)
         nc.vector.tensor_copy(columns[:], turned[:])
@@ -69,7 +67,7 @@ def tile_edgenetwork_kernel(
 
         for k in range(PIECES):
             cols = slice(k * PIECE, (k + 1) * PIECE)
-            layer1 = psum1.tile([P, PIECE], F32, name="layer1")
+            layer1 = psum.tile([P, PIECE], F32, name="layer1")
             if k == LAST:
                 nc.tensor.matmul(layer1[:], w1_sb[:], x[:, cols], start=True, stop=False)
                 nc.tensor.matmul(layer1[:], w_edge_row[:], edge_tail[:], start=False, stop=True)
@@ -78,7 +76,7 @@ def tile_edgenetwork_kernel(
                 nc.tensor.matmul(layer1[:], w1_sb[:], x[:, cols], start=True, stop=True)
                 nc.vector.scalar_tensor_tensor(pre[:, cols], edge_rows[:, cols], w_edge_col, layer1[:], MULT, ADD)
                 nc.scalar.activation(h[:, cols], pre[:, cols], RELU, bias=b1_col)
-            layer2 = psum2.tile([P, PIECE], F32, name="layer2")
+            layer2 = psum.tile([P, PIECE], F32, name="layer2")
             nc.tensor.matmul(layer2[:], w2_sb[:], h[:, cols], start=True, stop=True)
             if k % 2 == 1:
                 nc.vector.tensor_copy(y[:, cols], layer2[:])

@@ -32,9 +32,9 @@ def tile_edgenetwork_kernel(
         w1_sb = held.tile([P, P], BF16, name="w1_sb")
         w2_sb = held.tile([P, P], BF16, name="w2_sb")
         w_edge_row = held.tile([1, P], F32, name="w_edge_row")
-        b1_row = held.tile([1, P], F32, name="b1_row")
+        w_edge_col = held.tile([P, 1], F32, name="w_edge_col")
         one = held.tile([1, 1], F32, name="one")
-        columns = held.tile([P, 2], F32, name="columns")
+        b1_col = held.tile([P, 1], F32, name="b1_col")
         b2_col = held.tile([P, 1], F32, name="b2_col")
         pre = held.tile([P, SPREAD], F32, name="pre")
         h = held.tile([P, N], BF16, name="h")
@@ -47,7 +47,7 @@ def tile_edgenetwork_kernel(
         nc.sync.dma_start(x[64:80, :], src_feat)
         nc.scalar.dma_start(w_edge_row[:], w_edge.rearrange("m o -> o m"))
         nc.sync.dma_start(x[16:64, :], dst_hidden)
-        nc.scalar.dma_start(b1_row[:], b1.rearrange("m o -> o m"))
+        nc.scalar.dma_start(b1_col[:], b1)
         nc.scalar.dma_start(x[80:128, :], src_hidden)
         nc.scalar.dma_start(edge_rows[:], edge_feat[:, 0:SPREAD].broadcast_to([P, SPREAD]))
         nc.scalar.dma_start(w2_sb[:], w2)
@@ -56,12 +56,9 @@ def tile_edgenetwork_kernel(
         nc.sync.dma_start(window[:], base)
 
         nc.vector.memset(one[:], 1.0)
-        turned = psum.tile([P, 2], F32, name="turned", tag="layer2")
-        nc.tensor.matmul(turned[:, 0:1], w_edge_row[:], one[:], start=True, stop=True)
-        nc.tensor.matmul(turned[:, 1:2], b1_row[:], one[:], start=True, stop=True)
-        nc.vector.tensor_copy(columns[:], turned[:])
-        w_edge_col = columns[:, 0:1]
-        b1_col = columns[:, 1:2]
+        w_edge_turned = psum.tile([P, 1], F32, name="w_edge_turned", tag="layer2")
+        nc.tensor.matmul(w_edge_turned[:], w_edge_row[:], one[:], start=True, stop=True)
+        nc.vector.tensor_copy(w_edge_col[:], w_edge_turned[:])
 
         nc.gpsimd.tensor_copy(b2_rows[:], b2_col[:].to_broadcast([P, N]))
 
@@ -71,11 +68,11 @@ def tile_edgenetwork_kernel(
             if k == LAST:
                 nc.tensor.matmul(layer1[:], w1_sb[:], x[:, cols], start=True, stop=False)
                 nc.tensor.matmul(layer1[:], w_edge_row[:], edge_tail[:], start=False, stop=True)
-                nc.vector.tensor_scalar(h[:, cols], layer1[:], b1_col, 0.0, ADD, MAX)
+                nc.vector.tensor_scalar(h[:, cols], layer1[:], b1_col[:], 0.0, ADD, MAX)
             else:
                 nc.tensor.matmul(layer1[:], w1_sb[:], x[:, cols], start=True, stop=True)
-                nc.vector.scalar_tensor_tensor(pre[:, cols], edge_rows[:, cols], w_edge_col, layer1[:], MULT, ADD)
-                nc.scalar.activation(h[:, cols], pre[:, cols], RELU, bias=b1_col)
+                nc.vector.scalar_tensor_tensor(pre[:, cols], edge_rows[:, cols], w_edge_col[:], layer1[:], MULT, ADD)
+                nc.scalar.activation(h[:, cols], pre[:, cols], RELU, bias=b1_col[:])
             layer2 = psum.tile([P, PIECE], F32, name="layer2")
             nc.tensor.matmul(layer2[:], w2_sb[:], h[:, cols], start=True, stop=True)
             if k % 2 == 1:

import concourse.mybir as mybir

F32, BF16, U16 = mybir.dt.float32, mybir.dt.bfloat16, mybir.dt.uint16
ADD, MULT, MAX = mybir.AluOpType.add, mybir.AluOpType.mult, mybir.AluOpType.max
RELU = mybir.ActivationFunctionType.Relu

P = 128
N = 2048
S = 4096
PIECE = 512
PIECES = N // PIECE
LAST = PIECES - 1
SPREAD = LAST * PIECE

FLOPS = 2 * N * (P * P + P + P * P)
BYTES = 4 * P * S + 4 * P * (S - N) + 2 * P * N + 4 * N + 2 * 2 * P * P + 3 * 4 * P + 2 * P * (N // 16)


def tile_edgenetwork_kernel(
    tc, base, dst_feat, dst_hidden, src_feat, src_hidden, edge_feat, w1, w_edge, b1, w2, b2, offs, out
):
    nc = tc.nc
    with (
        tc.tile_pool(name="held", bufs=1) as held,
        tc.psum_pool(name="psum", bufs=PIECES) as psum,
    ):
        offsets = held.tile([P, N // 16], U16, name="offsets")
        window = held.tile([P, S], F32, name="window")
        x = held.tile([P, N], BF16, name="x")
        edge_rows = held.tile([P, SPREAD], F32, name="edge_rows")
        edge_tail = held.tile([1, PIECE], F32, name="edge_tail")
        w1_sb = held.tile([P, P], BF16, name="w1_sb")
        w2_sb = held.tile([P, P], BF16, name="w2_sb")
        w_edge_row = held.tile([1, P], F32, name="w_edge_row")
        w_edge_col = held.tile([P, 1], F32, name="w_edge_col")
        one = held.tile([1, 1], F32, name="one")
        b1_col = held.tile([P, 1], F32, name="b1_col")
        b2_col = held.tile([P, 1], F32, name="b2_col")
        pre = held.tile([P, SPREAD], F32, name="pre")
        h = held.tile([P, N], BF16, name="h")
        y = held.tile([P, N], F32, name="y")
        b2_rows = held.tile([P, N], F32, name="b2_rows")

        nc.gpsimd.dma_start(b2_col[:], b2)
        nc.sync.dma_start(x[0:16, :], dst_feat)
        nc.scalar.dma_start(w1_sb[:], w1)
        nc.sync.dma_start(x[64:80, :], src_feat)
        nc.scalar.dma_start(w_edge_row[:], w_edge.rearrange("m o -> o m"))
        nc.sync.dma_start(x[16:64, :], dst_hidden)
        nc.scalar.dma_start(b1_col[:], b1)
        nc.scalar.dma_start(x[80:128, :], src_hidden)
        nc.scalar.dma_start(edge_rows[:], edge_feat[:, 0:SPREAD].broadcast_to([P, SPREAD]))
        nc.scalar.dma_start(w2_sb[:], w2)
        nc.sync.dma_start(edge_tail[:], edge_feat[:, SPREAD:N])
        nc.sync.dma_start(offsets[:], offs)
        nc.sync.dma_start(window[:], base)

        nc.vector.memset(one[:], 1.0)
        w_edge_turned = psum.tile([P, 1], F32, name="w_edge_turned", tag="layer2")
        nc.tensor.matmul(w_edge_turned[:], w_edge_row[:], one[:], start=True, stop=True)
        nc.vector.tensor_copy(w_edge_col[:], w_edge_turned[:])

        nc.gpsimd.tensor_copy(b2_rows[:], b2_col[:].to_broadcast([P, N]))

        for k in range(PIECES):
            cols = slice(k * PIECE, (k + 1) * PIECE)
            layer1 = psum.tile([P, PIECE], F32, name="layer1")
            if k == LAST:
                nc.tensor.matmul(layer1[:], w1_sb[:], x[:, cols], start=True, stop=False)
                nc.tensor.matmul(layer1[:], w_edge_row[:], edge_tail[:], start=False, stop=True)
                nc.vector.tensor_scalar(h[:, cols], layer1[:], b1_col[:], 0.0, ADD, MAX)
            else:
                nc.tensor.matmul(layer1[:], w1_sb[:], x[:, cols], start=True, stop=True)
                nc.vector.scalar_tensor_tensor(pre[:, cols], edge_rows[:, cols], w_edge_col[:], layer1[:], MULT, ADD)
                nc.scalar.activation(h[:, cols], pre[:, cols], RELU, bias=b1_col[:])
            layer2 = psum.tile([P, PIECE], F32, name="layer2")
            nc.tensor.matmul(layer2[:], w2_sb[:], h[:, cols], start=True, stop=True)
            if k % 2 == 1:
                nc.vector.tensor_copy(y[:, cols], layer2[:])
            else:
                nc.scalar.copy(y[:, cols], layer2[:])

        nc.vector.tensor_tensor(window[:].indirect(offsets[:]), y[:], b2_rows[:], ADD)

        nc.sync.dma_start(out[:, 0 : S // 2], window[:, 0 : S // 2])
        nc.scalar.dma_start(out[:, S // 2 : S], window[:, S // 2 : S])
